import numpy as np
import ml_dtypes


def mxq(x, axis, fmt="e4m3"):
    dtype, down = {"e4m3": (ml_dtypes.float8_e4m3fn, 7), "e5m2": (ml_dtypes.float8_e5m2, 14)}[fmt]
    v = np.moveaxis(np.asarray(x, np.float32).astype(ml_dtypes.bfloat16).astype(np.float64), axis, -1)
    blocks = v.reshape(v.shape[:-1] + (-1, 32))
    amax = np.abs(blocks).max(-1, keepdims=True)
    byte = np.maximum(np.where(amax > 0, np.frexp(amax)[1] - 1 + 127, 0) - down, 1)
    scale = np.exp2(byte - 127.0)
    codes = (blocks / scale).astype(np.float32).astype(dtype).astype(np.float64)
    return np.moveaxis((codes * scale).reshape(v.shape), -1, axis)


WIDE = False


def mx_kscale(k):
    if not WIDE:
        return np.ones(k)
    levels = np.array([10, -10, 5, -5, 0])
    a = np.random.permutation(np.resize(levels, k // 512 * 4)).reshape(k // 512, 4)
    idx = np.arange(k)
    return np.exp2(a[idx // 512, idx % 128 // 32])


BF16 = ml_dtypes.bfloat16


def bf(x):
    return np.asarray(x, np.float32).astype(BF16)


def f64(x):
    return np.asarray(x).astype(np.float64)


B, D, H = 1024, 512, 1024


def sigmoid(v):
    return 1.0 / (1.0 + np.exp(-v))


def setup_inputs():
    s = mx_kscale(D)
    return {"x": bf(np.random.standard_normal((B, D)) * s),
            "W_ih0": bf(np.random.standard_normal((4 * H, D)) * 1.5 / np.sqrt(D) / s[None, :]),
            "b_ih0": bf(np.random.standard_normal(4 * H) * 0.3),
            "b_hh0": bf(np.random.standard_normal(4 * H) * 0.3)}


def reference(x, W_ih0, b_ih0, b_hh0):
    w = f64(W_ih0)
    b = f64(b_ih0) + f64(b_hh0)
    xq = mxq(f64(x), 1, "e4m3")
    a_i = (xq @ mxq(w[:H].T, 0, "e4m3")) + b[:H]
    a_go = (xq @ mxq(w[2 * H:].T, 0, "e4m3")) + b[2 * H:]
    a_g, a_o = a_go[:, :H], a_go[:, H:]
    c = sigmoid(a_i) * np.tanh(a_g)
    return sigmoid(a_o) * np.tanh(c)

@@ -1,0 +1,249 @@
+from contextlib import ExitStack
+
+import concourse.mybir as mybir
+from concourse.masks import make_identity
+
+F32 = mybir.dt.float32
+BF16 = mybir.dt.bfloat16
+U32 = mybir.dt.uint32
+U8 = mybir.dt.uint8
+FP8X4 = mybir.dt.float8_e4m3fn_x4
+AF = mybir.ActivationFunctionType
+ALU = mybir.AluOpType
+
+P = 128
+B, D, H = 1024, 512, 1024
+FLOPS = 2 * B * D * 3 * H
+BYTES = B * D * 2 + 3 * H * D * 2 + 2 * 3 * H * 2 + B * H * 4
+
+NB = B // P
+NH = H // P
+GATE_ROW_TILE = (0, 16, 24)
+
+
+def tile_lstmbaseline_pa_kernel(tc, x, W_ih0, b_ih0, b_hh0, out):
+    nc = tc.nc
+    with ExitStack() as ctx:
+        keep = ctx.enter_context(tc.tile_pool(name="keep", bufs=1))
+        work = ctx.enter_context(tc.tile_pool(name="work", bufs=3))
+        psum = ctx.enter_context(tc.psum_pool(name="psum", bufs=1))
+        ctx.enter_context(tc.manual_schedule())
+
+        x_sb = keep.tile([P, NB * D], BF16, name="x_sb")
+        w_sb = keep.tile([P, 3 * NH * D], BF16, name="w_sb")
+        xq = keep.tile([P, B], U32, name="xq", align_bytes=64)
+        xs = keep.tile([P, B], U8, name="xs", align_bytes=64)
+        wq = keep.tile([P, 3 * H], U32, name="wq", align_bytes=64)
+        ws = keep.tile([P, 3 * H], U8, name="ws", align_bytes=64)
+        out_sb = keep.tile([P, NB, H], F32, name="out_sb")
+        ident = keep.tile([P, P], F32, name="ident")
+        bsum = keep.tile([P, P], F32, name="bsum")
+        bih = keep.tile([32, P], BF16, name="bih")
+        bhh = keep.tile([32, P], BF16, name="bhh")
+        bias_sb = keep.tile([P, 32], F32, name="bias_sb")
+        warm_in = keep.tile([P, 1], F32, name="warm_in")
+        warm_out = keep.tile([P, 1], F32, name="warm_out")
+
+        x_view = x.rearrange("(p t) k -> p (t k)", t=NB)
+        out_view = out.rearrange("(p t) h -> p t h", t=NB)
+        x_words = x_sb[:].bitcast(F32)
+        w_words = w_sb[:].bitcast(F32)
+
+        def bank(tag):
+            return psum.tile([P, 512], F32, name="ps_" + tag, tag=tag)
+
+        def load_x(pair):
+            cols = slice(pair * 2 * D, (pair + 1) * 2 * D)
+            nc.sync.dma_start(out=x_sb[:, cols], in_=x_view[:, cols])
+
+        def load_w(gi, hp):
+            slot = gi * NH + 2 * hp
+            row = (GATE_ROW_TILE[gi] + 2 * hp) * P
+            nc.sync.dma_start(
+                out=w_sb[:, slot * D : (slot + 2) * D].rearrange("p (t k) -> p t k", t=2),
+                in_=W_ih0[row : row + 2 * P, :].rearrange("(t p) k -> p t k", p=P),
+            )
+
+        def job_words(job):
+            kind, a, b2 = job
+            if kind == "x":
+                return x_words, a * 2
+            return w_words, a * NH + 2 * b2
+
+        def prep_transpose(job, tag):
+            words, first = job_words(job)
+            ps = bank(tag)
+            for r in range(2):
+                for u in range(2):
+                    src = (first + r) * 256 + u * P
+                    nc.tensor.transpose(
+                        ps[:, u * 256 + r * P : u * 256 + (r + 1) * P], words[:, src : src + P], ident[:]
+                    )
+            return ps
+
+        def prep_copy(engine, ps):
+            grouped = work.tile([P, 1024], BF16, name="grouped", tag="grouped", align_bytes=64)
+            dst = grouped[:].bitcast(F32).rearrange("p (c u) -> p c u", u=2)
+            src = ps[:].rearrange("p (u c) -> p c u", u=2)
+            if engine == "v":
+                nc.vector.tensor_copy(out=dst, in_=src)
+            else:
+                nc.scalar.copy(out=dst, in_=src)
+            return grouped
+
+        def prep_quant(job, grouped):
+            kind, a, b2 = job
+            if kind == "x":
+                codes, scales, c0 = xq, xs, a * 256
+            else:
+                codes, scales, c0 = wq, ws, (a * NH + 2 * b2) * P
+            nc.vector.quantize_mx(
+                out=codes[:, c0 : c0 + 256].bitcast(FP8X4), scales=scales[:, c0 : c0 + 256], in_=grouped[:]
+            )
+
+        units = []
+        for hp in range(NH // 2):
+            for grp in range(2):
+                for ht in (2 * hp, 2 * hp + 1):
+                    units.append((ht, grp))
+        NU = len(units)
+        mx_ps = {}
+        acts = {}
+        c_t = {}
+        c_ps = {}
+        o_ps = {}
+        th = {}
+
+        def mx(n):
+            ht, grp = units[n]
+            for gi in range(3):
+                ps = bank("m%d" % ((3 * n + gi) % 4))
+                slot = gi * NH + ht
+                nc.tensor.matmul_mx(
+                    out=ps[:],
+                    lhsT=wq[:, slot * P : (slot + 1) * P].bitcast(FP8X4),
+                    lhsT_scale=ws[:, slot * P : (slot + 1) * P],
+                    rhs=xq[:, grp * 512 : (grp + 1) * 512].bitcast(FP8X4),
+                    rhs_scale=xs[:, grp * 512 : (grp + 1) * 512],
+                    start=True,
+                    stop=True,
+                )
+                mx_ps[(n, gi)] = ps
+
+        def act_gate(n, gi):
+            ht, grp = units[n]
+            res = work.tile([P, 512], F32, name="gate%d" % gi, tag="gate%d" % gi)
+            col = GATE_ROW_TILE[gi] + ht
+            nc.scalar.activation(
+                out=res[:],
+                in_=mx_ps[(n, gi)][:],
+                func=AF.Tanh if gi == 1 else AF.Sigmoid,
+                bias=bias_sb[:, col : col + 1],
+                scale=1.0,
+            )
+            acts[(n, gi)] = res
+
+        def cmult(n):
+            res = work.tile([P, 512], F32, name="c_t", tag="c_t")
+            nc.vector.tensor_tensor(out=res[:], in0=acts[(n, 0)][:], in1=acts[(n, 1)][:], op=ALU.mult)
+            c_t[n] = res
+
+        def back_transpose(src, tag):
+            ps = bank(tag)
+            for tl in range(4):
+                nc.tensor.transpose(ps[:, tl * P : (tl + 1) * P], src[:, tl * P : (tl + 1) * P], ident[:])
+            return ps
+
+        def act_c(n):
+            res = work.tile([P, 512], F32, name="th", tag="th")
+            nc.scalar.activation(out=res[:], in_=c_ps[n][:], func=AF.Tanh)
+            th[n] = res
+
+        def final(n):
+            ht, grp = units[n]
+            nc.vector.tensor_tensor(
+                out=out_sb[:, 4 * grp : 4 * grp + 4, ht * P : (ht + 1) * P],
+                in0=o_ps[n][:].rearrange("p (t m) -> p t m", t=4),
+                in1=th[n][:].rearrange("p (t m) -> p t m", t=4),
+                op=ALU.mult,
+            )
+
+        def store(grp, h0, h1):
+            nc.sync.dma_start(
+                out=out_view[:, 4 * grp : 4 * grp + 4, h0:h1], in_=out_sb[:, 4 * grp : 4 * grp + 4, h0:h1]
+            )
+
+        nc.scalar.dma_start(out=bih[:], in_=b_ih0.rearrange("(t p) -> t p", p=P))
+        nc.scalar.dma_start(out=bhh[:], in_=b_hh0.rearrange("(t p) -> t p", p=P))
+        load_x(0)
+        load_x(1)
+        for gi in range(3):
+            load_w(gi, 0)
+        load_x(2)
+        load_x(3)
+        for hp in range(1, NH // 2):
+            for gi in range(3):
+                load_w(gi, hp)
+
+        make_identity(nc, ident[:])
+        nc.vector.memset(warm_in[:], 0.0)
+        nc.vector.memset(bsum[:], 0.0)
+        nc.scalar.activation(out=warm_out[:], in_=warm_in[:], func=AF.Sigmoid)
+
+        jx0, jx1 = ("x", 0, 0), ("x", 1, 0)
+        jw = [("w", gi, 0) for gi in range(3)]
+        p_x0 = prep_transpose(jx0, "in0")
+        p_x1 = prep_transpose(jx1, "o0")
+        nc.vector.tensor_tensor(out=bsum[0:32, :], in0=bih[:], in1=bhh[:], op=ALU.add)
+        p_b = bank("m3")
+        nc.tensor.transpose(p_b[:, 0:P], bsum[:], ident[:])
+        g_x0 = prep_copy("v", p_x0)
+        g_x1 = prep_copy("s", p_x1)
+        p_w0 = prep_transpose(jw[0], "o1")
+        p_w1 = prep_transpose(jw[1], "c0")
+        prep_quant(jx0, g_x0)
+        nc.vector.tensor_copy(out=bias_sb[:], in_=p_b[:, 0:32])
+        prep_quant(jx1, g_x1)
+        g_w0 = prep_copy("v", p_w0)
+        g_w1 = prep_copy("s", p_w1)
+        p_w2 = prep_transpose(jw[2], "in0")
+        prep_quant(jw[0], g_w0)
+        prep_quant(jw[1], g_w1)
+        g_w2 = prep_copy("v", p_w2)
+        prep_quant(jw[2], g_w2)
+        mx(0)
+
+        jobs = {0: [(("x", 2, 0), "o0"), (("x", 3, 0), "o1")], 1: [(("w", 0, 1), "in0"), (("w", 1, 1), "o1")], 2: [(("w", 2, 1), "in0")]}
+        for hp in (2, 3):
+            for gi in range(3):
+                jobs[4 * hp - 4 + gi] = [(("w", gi, hp), "in0")]
+
+        pending = []
+        for n in range(NU + 2):
+            if n >= 2:
+                final(n - 2)
+                ht, grp = units[n - 2]
+                if n - 2 >= NU - 2:
+                    store(grp, ht * P, (ht + 1) * P)
+                elif ht % 2 == 1:
+                    store(grp, (ht - 1) * P, (ht + 1) * P)
+            for job, grouped in pending:
+                prep_quant(job, grouped)
+            pending = []
+            if 1 <= n <= NU:
+                o_ps[n - 1] = back_transpose(acts[(n - 1, 2)], "o%d" % ((n - 1) % 2))
+                c_ps[n - 1] = back_transpose(c_t[n - 1], "c0")
+            banks = [(job, prep_transpose(job, tag)) for job, tag in jobs.get(n, [])]
+            if n < NU:
+                act_gate(n, 0)
+                act_gate(n, 1)
+            if n + 1 < NU:
+                mx(n + 1)
+            if n < NU:
+                act_gate(n, 2)
+            if 1 <= n <= NU:
+                act_c(n - 1)
+            if n < NU:
+                cmult(n)
+            for job, ps in banks:
+                pending.append((job, prep_copy("v", ps)))

@@ -145,7 +145,8 @@ def tile_lstmbaseline_pa_kernel(tc, x, W_ih0, b_ih0, b_hh0, out):
 
         def cmult(n):
             res = work.tile([P, 512], F32, name="c_t", tag="c_t")
-            nc.vector.tensor_tensor(out=res[:], in0=acts[(n, 0)][:], in1=acts[(n, 1)][:], op=ALU.mult)
+            engine = nc.gpsimd if n < NU - 2 else nc.vector
+            engine.tensor_tensor(out=res[:], in0=acts[(n, 0)][:], in1=acts[(n, 1)][:], op=ALU.mult)
             c_t[n] = res
 
         def back_transpose(src, tag):
@@ -232,8 +233,9 @@ def tile_lstmbaseline_pa_kernel(tc, x, W_ih0, b_ih0, b_hh0, out):
             pending = []
             if 1 <= n <= NU:
                 o_ps[n - 1] = back_transpose(acts[(n - 1, 2)], "o%d" % ((n - 1) % 2))
-                c_ps[n - 1] = back_transpose(c_t[n - 1], "c0")
             banks = [(job, prep_transpose(job, tag)) for job, tag in jobs.get(n, [])]
+            if 1 <= n <= NU:
+                c_ps[n - 1] = back_transpose(c_t[n - 1], "c0")
             if n < NU:
                 act_gate(n, 0)
                 act_gate(n, 1)

@@ -19,6 +19,7 @@ BYTES = B * D * 2 + 3 * H * D * 2 + 2 * 3 * H * 2 + B * H * 4
 NB = B // P
 NH = H // P
 GATE_ROW_TILE = (0, 16, 24)
+WARM = 0
 
 
 def tile_lstmbaseline_pa_kernel(tc, x, W_ih0, b_ih0, b_hh0, out):
@@ -52,16 +53,23 @@ def tile_lstmbaseline_pa_kernel(tc, x, W_ih0, b_ih0, b_hh0, out):
         def bank(tag):
             return psum.tile([P, 512], F32, name="ps_" + tag, tag=tag)
 
+        mx_count = [0]
+
+        def mx_bank():
+            tag = "m%d" % (mx_count[0] % 4)
+            mx_count[0] += 1
+            return bank(tag)
+
         def load_x(pair):
             cols = slice(pair * 2 * D, (pair + 1) * 2 * D)
             nc.sync.dma_start(out=x_sb[:, cols], in_=x_view[:, cols])
 
-        def load_w(gi, hp):
-            slot = gi * NH + 2 * hp
-            row = (GATE_ROW_TILE[gi] + 2 * hp) * P
+        def load_w(gi, ht, count):
+            slot = gi * NH + ht
+            row = (GATE_ROW_TILE[gi] + ht) * P
             nc.sync.dma_start(
-                out=w_sb[:, slot * D : (slot + 2) * D].rearrange("p (t k) -> p t k", t=2),
-                in_=W_ih0[row : row + 2 * P, :].rearrange("(t p) k -> p t k", p=P),
+                out=w_sb[:, slot * D : (slot + count) * D].rearrange("p (t k) -> p t k", t=count),
+                in_=W_ih0[row : row + count * P, :].rearrange("(t p) k -> p t k", p=P),
             )
 
         def job_words(job):
@@ -82,7 +90,7 @@ def tile_lstmbaseline_pa_kernel(tc, x, W_ih0, b_ih0, b_hh0, out):
             return ps
 
         def prep_copy(engine, ps):
-            grouped = work.tile([P, 1024], BF16, name="grouped", tag="grouped", align_bytes=64)
+            grouped = work.tile([P, 1024], BF16, name="grouped", tag="grouped", bufs=4, align_bytes=64)
             dst = grouped[:].bitcast(F32).rearrange("p (c u) -> p c u", u=2)
             src = ps[:].rearrange("p (u c) -> p c u", u=2)
             if engine == "v":
@@ -107,145 +115,189 @@ def tile_lstmbaseline_pa_kernel(tc, x, W_ih0, b_ih0, b_hh0, out):
                 for ht in (2 * hp, 2 * hp + 1):
                     units.append((ht, grp))
         NU = len(units)
-        mx_ps = {}
         acts = {}
         c_t = {}
         c_ps = {}
         o_ps = {}
         th = {}
 
-        def mx(n):
+        def mx_pass(n, gi, c0, c1):
             ht, grp = units[n]
-            for gi in range(3):
-                ps = bank("m%d" % ((3 * n + gi) % 4))
-                slot = gi * NH + ht
-                nc.tensor.matmul_mx(
-                    out=ps[:],
-                    lhsT=wq[:, slot * P : (slot + 1) * P].bitcast(FP8X4),
-                    lhsT_scale=ws[:, slot * P : (slot + 1) * P],
-                    rhs=xq[:, grp * 512 : (grp + 1) * 512].bitcast(FP8X4),
-                    rhs_scale=xs[:, grp * 512 : (grp + 1) * 512],
-                    start=True,
-                    stop=True,
-                )
-                mx_ps[(n, gi)] = ps
+            ps = mx_bank()
+            slot = gi * NH + ht
+            cols = slice(grp * 512 + c0, grp * 512 + c1)
+            nc.tensor.matmul_mx(
+                out=ps[:, 0 : c1 - c0],
+                lhsT=wq[:, slot * P : (slot + 1) * P].bitcast(FP8X4),
+                lhsT_scale=ws[:, slot * P : (slot + 1) * P],
+                rhs=xq[:, cols].bitcast(FP8X4),
+                rhs_scale=xs[:, cols],
+                start=True,
+                stop=True,
+            )
+            return ps
 
-        def act_gate(n, gi):
+        def act_gate(n, gi, ps, c0, c1):
             ht, grp = units[n]
-            res = work.tile([P, 512], F32, name="gate%d" % gi, tag="gate%d" % gi)
+            if (n, gi) not in acts:
+                acts[(n, gi)] = work.tile([P, 512], F32, name="gate%d" % gi, tag="gate%d" % gi)
             col = GATE_ROW_TILE[gi] + ht
             nc.scalar.activation(
-                out=res[:],
-                in_=mx_ps[(n, gi)][:],
+                out=acts[(n, gi)][:, c0:c1],
+                in_=ps[:, 0 : c1 - c0],
                 func=AF.Tanh if gi == 1 else AF.Sigmoid,
                 bias=bias_sb[:, col : col + 1],
                 scale=1.0,
             )
-            acts[(n, gi)] = res
 
-        def cmult(n):
-            res = work.tile([P, 512], F32, name="c_t", tag="c_t")
-            engine = nc.gpsimd if n < NU - 2 else nc.vector
-            engine.tensor_tensor(out=res[:], in0=acts[(n, 0)][:], in1=acts[(n, 1)][:], op=ALU.mult)
-            c_t[n] = res
+        def cmult(engine, n, c0, c1):
+            if n not in c_t:
+                c_t[n] = work.tile([P, 512], F32, name="c_t", tag="c_t")
+            engine.tensor_tensor(
+                out=c_t[n][:, c0:c1], in0=acts[(n, 0)][:, c0:c1], in1=acts[(n, 1)][:, c0:c1], op=ALU.mult
+            )
 
-        def back_transpose(src, tag):
-            ps = bank(tag)
-            for tl in range(4):
-                nc.tensor.transpose(ps[:, tl * P : (tl + 1) * P], src[:, tl * P : (tl + 1) * P], ident[:])
+        def back_transpose(src, ps, t0, t1):
+            for tl in range(t0, t1):
+                nc.tensor.transpose(
+                    ps[:, (tl - t0) * P : (tl - t0 + 1) * P], src[:, tl * P : (tl + 1) * P], ident[:]
+                )
             return ps
 
-        def act_c(n):
-            res = work.tile([P, 512], F32, name="th", tag="th")
-            nc.scalar.activation(out=res[:], in_=c_ps[n][:], func=AF.Tanh)
-            th[n] = res
+        def act_c(n, ps, c0, c1):
+            if n not in th:
+                th[n] = work.tile([P, 512], F32, name="th", tag="th")
+            nc.scalar.activation(out=th[n][:, c0:c1], in_=ps[:, 0 : c1 - c0], func=AF.Tanh)
 
-        def final(n):
+        def final(n, t0, t1):
             ht, grp = units[n]
             nc.vector.tensor_tensor(
-                out=out_sb[:, 4 * grp : 4 * grp + 4, ht * P : (ht + 1) * P],
-                in0=o_ps[n][:].rearrange("p (t m) -> p t m", t=4),
-                in1=th[n][:].rearrange("p (t m) -> p t m", t=4),
+                out=out_sb[:, 4 * grp + t0 : 4 * grp + t1, ht * P : (ht + 1) * P],
+                in0=o_ps[n][:, t0 * P : t1 * P].rearrange("p (t m) -> p t m", m=P),
+                in1=th[n][:, t0 * P : t1 * P].rearrange("p (t m) -> p t m", m=P),
                 op=ALU.mult,
             )
 
-        def store(grp, h0, h1):
-            nc.sync.dma_start(
-                out=out_view[:, 4 * grp : 4 * grp + 4, h0:h1], in_=out_sb[:, 4 * grp : 4 * grp + 4, h0:h1]
-            )
+        def store(t0, t1, h0, h1):
+            nc.sync.dma_start(out=out_view[:, t0:t1, h0:h1], in_=out_sb[:, t0:t1, h0:h1])
 
         nc.scalar.dma_start(out=bih[:], in_=b_ih0.rearrange("(t p) -> t p", p=P))
         nc.scalar.dma_start(out=bhh[:], in_=b_hh0.rearrange("(t p) -> t p", p=P))
+        load_w(0, 0, 1)
+        load_w(0, 1, 1)
         load_x(0)
         load_x(1)
-        for gi in range(3):
-            load_w(gi, 0)
+        load_w(1, 0, 2)
+        load_w(2, 0, 2)
         load_x(2)
         load_x(3)
         for hp in range(1, NH // 2):
             for gi in range(3):
-                load_w(gi, hp)
+                load_w(gi, 2 * hp, 2)
 
         make_identity(nc, ident[:])
         nc.vector.memset(warm_in[:], 0.0)
         nc.vector.memset(bsum[:], 0.0)
         nc.scalar.activation(out=warm_out[:], in_=warm_in[:], func=AF.Sigmoid)
+        if WARM:
+            zeros = keep.tile([P, 512], BF16, name="zeros")
+            nc.vector.memset(zeros[:], 0.0)
+            ps_warm = bank("m3")
+            for k in range(WARM):
+                nc.tensor.matmul(out=ps_warm[:], lhsT=zeros[:, 0:P], rhs=zeros[:], start=True, stop=True)
 
-        jx0, jx1 = ("x", 0, 0), ("x", 1, 0)
-        jw = [("w", gi, 0) for gi in range(3)]
-        p_x0 = prep_transpose(jx0, "in0")
-        p_x1 = prep_transpose(jx1, "o0")
+        j_w = [("w", gi, 0) for gi in range(3)]
+        j_x = [("x", k, 0) for k in range(4)]
+        p_wi = prep_transpose(j_w[0], "o1")
+        p_x0 = prep_transpose(j_x[0], "in0")
+        p_x1 = prep_transpose(j_x[1], "o0")
         nc.vector.tensor_tensor(out=bsum[0:32, :], in0=bih[:], in1=bhh[:], op=ALU.add)
-        p_b = bank("m3")
+        p_b = bank("c0")
         nc.tensor.transpose(p_b[:, 0:P], bsum[:], ident[:])
-        g_x0 = prep_copy("v", p_x0)
+        g_wi = prep_copy("v", p_wi)
+        g_x0 = prep_copy("s", p_x0)
+        prep_quant(j_w[0], g_wi)
         g_x1 = prep_copy("s", p_x1)
-        p_w0 = prep_transpose(jw[0], "o1")
-        p_w1 = prep_transpose(jw[1], "c0")
-        prep_quant(jx0, g_x0)
+        prep_quant(j_x[0], g_x0)
         nc.vector.tensor_copy(out=bias_sb[:], in_=p_b[:, 0:32])
-        prep_quant(jx1, g_x1)
-        g_w0 = prep_copy("v", p_w0)
-        g_w1 = prep_copy("s", p_w1)
-        p_w2 = prep_transpose(jw[2], "in0")
-        prep_quant(jw[0], g_w0)
-        prep_quant(jw[1], g_w1)
-        g_w2 = prep_copy("v", p_w2)
-        prep_quant(jw[2], g_w2)
-        mx(0)
+        prep_quant(j_x[1], g_x1)
+        p_wg = prep_transpose(j_w[1], "o1")
+        g_wg = prep_copy("s", p_wg)
+        ia = [mx_pass(0, 0, 0, 256), mx_pass(1, 0, 0, 256)]
+        p_wo = prep_transpose(j_w[2], "in0")
+        ib = [mx_pass(0, 0, 256, 512), mx_pass(1, 0, 256, 512)]
+        act_gate(0, 0, ia[0], 0, 256)
+        act_gate(1, 0, ia[1], 0, 256)
+        act_gate(0, 0, ib[0], 256, 512)
+        act_gate(1, 0, ib[1], 256, 512)
+        prep_quant(j_w[1], g_wg)
+        g_wo = prep_copy("v", p_wo)
+        prep_quant(j_w[2], g_wo)
+        gg = [mx_pass(0, 1, 0, 512), mx_pass(1, 1, 0, 512)]
+        p_x2 = prep_transpose(j_x[2], "o0")
+        act_gate(0, 1, gg[0], 0, 512)
+        act_gate(1, 1, gg[1], 0, 512)
+        cmult(nc.gpsimd, 0, 0, 512)
+        cmult(nc.gpsimd, 1, 0, 512)
+        oo = [mx_pass(0, 2, 0, 512), mx_pass(1, 2, 0, 512)]
+        p_x3 = prep_transpose(j_x[3], "o1")
+        act_gate(0, 2, oo[0], 0, 512)
+        act_gate(1, 2, oo[1], 0, 512)
+        g_x2 = prep_copy("v", p_x2)
+        prep_quant(j_x[2], g_x2)
+        g_x3 = prep_copy("v", p_x3)
+        prep_quant(j_x[3], g_x3)
+        o_ps[0] = back_transpose(acts[(0, 2)], bank("o0"), 0, 4)
+        c_ps[0] = back_transpose(c_t[0], bank("c0"), 0, 4)
+        j_wi1 = ("w", 0, 1)
+        p_wi1 = prep_transpose(j_wi1, "in0")
+        act_c(0, c_ps[0], 0, 512)
+        nxt = [mx_pass(2, gi, 0, 512) for gi in range(3)]
+        pending = [(j_wi1, prep_copy("v", p_wi1))]
 
-        jobs = {0: [(("x", 2, 0), "o0"), (("x", 3, 0), "o1")], 1: [(("w", 0, 1), "in0"), (("w", 1, 1), "o1")], 2: [(("w", 2, 1), "in0")]}
+        jobs = {2: [(("w", 1, 1), "in0"), (("w", 2, 1), "o0")]}
         for hp in (2, 3):
             for gi in range(3):
                 jobs[4 * hp - 4 + gi] = [(("w", gi, hp), "in0")]
 
-        pending = []
-        for n in range(NU + 2):
-            if n >= 2:
-                final(n - 2)
-                ht, grp = units[n - 2]
-                if n - 2 >= NU - 2:
-                    store(grp, ht * P, (ht + 1) * P)
-                elif ht % 2 == 1:
-                    store(grp, (ht - 1) * P, (ht + 1) * P)
+        for n in range(2, NU):
             for job, grouped in pending:
                 prep_quant(job, grouped)
             pending = []
-            if 1 <= n <= NU:
-                o_ps[n - 1] = back_transpose(acts[(n - 1, 2)], "o%d" % ((n - 1) % 2))
+            final(n - 2, 0, 4)
+            ht, grp = units[n - 2]
+            if ht % 2 == 1:
+                store(4 * grp, 4 * grp + 4, (ht - 1) * P, (ht + 1) * P)
+            o_ps[n - 1] = back_transpose(acts[(n - 1, 2)], bank("o%d" % ((n - 1) % 2)), 0, 4)
             banks = [(job, prep_transpose(job, tag)) for job, tag in jobs.get(n, [])]
-            if 1 <= n <= NU:
-                c_ps[n - 1] = back_transpose(c_t[n - 1], "c0")
-            if n < NU:
-                act_gate(n, 0)
-                act_gate(n, 1)
+            c_ps[n - 1] = back_transpose(c_t[n - 1], bank("c0"), 0, 4)
+            cur = nxt
+            act_gate(n, 0, cur[0], 0, 512)
+            act_gate(n, 1, cur[1], 0, 512)
             if n + 1 < NU:
-                mx(n + 1)
-            if n < NU:
-                act_gate(n, 2)
-            if 1 <= n <= NU:
-                act_c(n - 1)
-            if n < NU:
-                cmult(n)
+                nxt = [mx_pass(n + 1, gi, 0, 512) for gi in range(3)]
+            act_gate(n, 2, cur[2], 0, 512)
+            act_c(n - 1, c_ps[n - 1], 0, 512)
+            if n < NU - 2:
+                cmult(nc.gpsimd, n, 0, 512)
+            elif n == NU - 2:
+                cmult(nc.vector, n, 0, 512)
+            else:
+                cmult(nc.vector, n, 0, 256)
+                cmult(nc.vector, n, 256, 512)
             for job, ps in banks:
                 pending.append((job, prep_copy("v", ps)))
+
+        last = NU - 1
+        ht, grp = units[last - 1]
+        final(last - 1, 0, 4)
+        store(4 * grp, 4 * grp + 4, ht * P, (ht + 1) * P)
+        ht, grp = units[last]
+        c_a = back_transpose(c_t[last], bank("in0"), 0, 2)
+        c_b = back_transpose(c_t[last], mx_bank(), 2, 4)
+        o_ps[last] = back_transpose(acts[(last, 2)], bank("o%d" % (last % 2)), 0, 4)
+        act_c(last, c_a, 0, 256)
+        act_c(last, c_b, 256, 512)
+        for t0 in (0, 2):
+            final(last, t0, t0 + 2)
+            store(4 * grp + t0, 4 * grp + t0 + 2, ht * P, (ht + 1) * P)

@@ -19,7 +19,7 @@ BYTES = B * D * 2 + 3 * H * D * 2 + 2 * 3 * H * 2 + B * H * 4
 NB = B // P
 NH = H // P
 GATE_ROW_TILE = (0, 16, 24)
-WARM = 0
+WARM = 5
 
 
 def tile_lstmbaseline_pa_kernel(tc, x, W_ih0, b_ih0, b_hh0, out):
@@ -203,14 +203,21 @@ def tile_lstmbaseline_pa_kernel(tc, x, W_ih0, b_ih0, b_hh0, out):
             zeros = keep.tile([P, 512], BF16, name="zeros")
             nc.vector.memset(zeros[:], 0.0)
             ps_warm = bank("m3")
-            for k in range(WARM):
+
+        def dummy(count):
+            for k in range(count):
                 nc.tensor.matmul(out=ps_warm[:], lhsT=zeros[:, 0:P], rhs=zeros[:], start=True, stop=True)
+
+        dummy(WARM)
 
         j_w = [("w", gi, 0) for gi in range(3)]
         j_x = [("x", k, 0) for k in range(4)]
         p_wi = prep_transpose(j_w[0], "o1")
+        dummy(1)
         p_x0 = prep_transpose(j_x[0], "in0")
+        dummy(1)
         p_x1 = prep_transpose(j_x[1], "o0")
+        dummy(1)
         nc.vector.tensor_tensor(out=bsum[0:32, :], in0=bih[:], in1=bhh[:], op=ALU.add)
         p_b = bank("c0")
         nc.tensor.transpose(p_b[:, 0:P], bsum[:], ident[:])

from contextlib import ExitStack

import concourse.mybir as mybir
from concourse.masks import make_identity

F32 = mybir.dt.float32
BF16 = mybir.dt.bfloat16
U32 = mybir.dt.uint32
U8 = mybir.dt.uint8
FP8X4 = mybir.dt.float8_e4m3fn_x4
AF = mybir.ActivationFunctionType
ALU = mybir.AluOpType

P = 128
B, D, H = 1024, 512, 1024
FLOPS = 2 * B * D * 3 * H
BYTES = B * D * 2 + 3 * H * D * 2 + 2 * 3 * H * 2 + B * H * 4

NB = B // P
NH = H // P
GATE_ROW_TILE = (0, 16, 24)
WARM = 5


def tile_lstmbaseline_pa_kernel(tc, x, W_ih0, b_ih0, b_hh0, out):
    nc = tc.nc
    with ExitStack() as ctx:
        keep = ctx.enter_context(tc.tile_pool(name="keep", bufs=1))
        work = ctx.enter_context(tc.tile_pool(name="work", bufs=3))
        psum = ctx.enter_context(tc.psum_pool(name="psum", bufs=1))
        ctx.enter_context(tc.manual_schedule())

        x_sb = keep.tile([P, NB * D], BF16, name="x_sb")
        w_sb = keep.tile([P, 3 * NH * D], BF16, name="w_sb")
        xq = keep.tile([P, B], U32, name="xq", align_bytes=64)
        xs = keep.tile([P, B], U8, name="xs", align_bytes=64)
        wq = keep.tile([P, 3 * H], U32, name="wq", align_bytes=64)
        ws = keep.tile([P, 3 * H], U8, name="ws", align_bytes=64)
        out_sb = keep.tile([P, NB, H], F32, name="out_sb")
        ident = keep.tile([P, P], F32, name="ident")
        bsum = keep.tile([P, P], F32, name="bsum")
        bih = keep.tile([32, P], BF16, name="bih")
        bhh = keep.tile([32, P], BF16, name="bhh")
        bias_sb = keep.tile([P, 32], F32, name="bias_sb")
        warm_in = keep.tile([P, 1], F32, name="warm_in")
        warm_out = keep.tile([P, 1], F32, name="warm_out")

        x_view = x.rearrange("(p t) k -> p (t k)", t=NB)
        out_view = out.rearrange("(p t) h -> p t h", t=NB)
        x_words = x_sb[:].bitcast(F32)
        w_words = w_sb[:].bitcast(F32)

        def bank(tag):
            return psum.tile([P, 512], F32, name="ps_" + tag, tag=tag)

        mx_count = [0]

        def mx_bank():
            tag = "m%d" % (mx_count[0] % 4)
            mx_count[0] += 1
            return bank(tag)

        def load_x(pair):
            cols = slice(pair * 2 * D, (pair + 1) * 2 * D)
            nc.sync.dma_start(out=x_sb[:, cols], in_=x_view[:, cols])

        def load_w(gi, ht, count):
            slot = gi * NH + ht
            row = (GATE_ROW_TILE[gi] + ht) * P
            nc.sync.dma_start(
                out=w_sb[:, slot * D : (slot + count) * D].rearrange("p (t k) -> p t k", t=count),
                in_=W_ih0[row : row + count * P, :].rearrange("(t p) k -> p t k", p=P),
            )

        def job_words(job):
            kind, a, b2 = job
            if kind == "x":
                return x_words, a * 2
            return w_words, a * NH + 2 * b2

        def prep_transpose(job, tag):
            words, first = job_words(job)
            ps = bank(tag)
            for r in range(2):
                for u in range(2):
                    src = (first + r) * 256 + u * P
                    nc.tensor.transpose(
                        ps[:, u * 256 + r * P : u * 256 + (r + 1) * P], words[:, src : src + P], ident[:]
                    )
            return ps

        def prep_copy(engine, ps):
            grouped = work.tile([P, 1024], BF16, name="grouped", tag="grouped", bufs=4, align_bytes=64)
            dst = grouped[:].bitcast(F32).rearrange("p (c u) -> p c u", u=2)
            src = ps[:].rearrange("p (u c) -> p c u", u=2)
            if engine == "v":
                nc.vector.tensor_copy(out=dst, in_=src)
            else:
                nc.scalar.copy(out=dst, in_=src)
            return grouped

        def prep_quant(job, grouped):
            kind, a, b2 = job
            if kind == "x":
                codes, scales, c0 = xq, xs, a * 256
            else:
                codes, scales, c0 = wq, ws, (a * NH + 2 * b2) * P
            nc.vector.quantize_mx(
                out=codes[:, c0 : c0 + 256].bitcast(FP8X4), scales=scales[:, c0 : c0 + 256], in_=grouped[:]
            )

        units = []
        for hp in range(NH // 2):
            for grp in range(2):
                for ht in (2 * hp, 2 * hp + 1):
                    units.append((ht, grp))
        NU = len(units)
        acts = {}
        c_t = {}
        c_ps = {}
        o_ps = {}
        th = {}

        def mx_pass(n, gi, c0, c1):
            ht, grp = units[n]
            ps = mx_bank()
            slot = gi * NH + ht
            cols = slice(grp * 512 + c0, grp * 512 + c1)
            nc.tensor.matmul_mx(
                out=ps[:, 0 : c1 - c0],
                lhsT=wq[:, slot * P : (slot + 1) * P].bitcast(FP8X4),
                lhsT_scale=ws[:, slot * P : (slot + 1) * P],
                rhs=xq[:, cols].bitcast(FP8X4),
                rhs_scale=xs[:, cols],
                start=True,
                stop=True,
            )
            return ps

        def act_gate(n, gi, ps, c0, c1):
            ht, grp = units[n]
            if (n, gi) not in acts:
                acts[(n, gi)] = work.tile([P, 512], F32, name="gate%d" % gi, tag="gate%d" % gi)
            col = GATE_ROW_TILE[gi] + ht
            nc.scalar.activation(
                out=acts[(n, gi)][:, c0:c1],
                in_=ps[:, 0 : c1 - c0],
                func=AF.Tanh if gi == 1 else AF.Sigmoid,
                bias=bias_sb[:, col : col + 1],
                scale=1.0,
            )

        def cmult(engine, n, c0, c1):
            if n not in c_t:
                c_t[n] = work.tile([P, 512], F32, name="c_t", tag="c_t")
            engine.tensor_tensor(
                out=c_t[n][:, c0:c1], in0=acts[(n, 0)][:, c0:c1], in1=acts[(n, 1)][:, c0:c1], op=ALU.mult
            )

        def back_transpose(src, ps, t0, t1):
            for tl in range(t0, t1):
                nc.tensor.transpose(
                    ps[:, (tl - t0) * P : (tl - t0 + 1) * P], src[:, tl * P : (tl + 1) * P], ident[:]
                )
            return ps

        def act_c(n, ps, c0, c1):
            if n not in th:
                th[n] = work.tile([P, 512], F32, name="th", tag="th")
            nc.scalar.activation(out=th[n][:, c0:c1], in_=ps[:, 0 : c1 - c0], func=AF.Tanh)

        def final(n, t0, t1):
            ht, grp = units[n]
            nc.vector.tensor_tensor(
                out=out_sb[:, 4 * grp + t0 : 4 * grp + t1, ht * P : (ht + 1) * P],
                in0=o_ps[n][:, t0 * P : t1 * P].rearrange("p (t m) -> p t m", m=P),
                in1=th[n][:, t0 * P : t1 * P].rearrange("p (t m) -> p t m", m=P),
                op=ALU.mult,
            )

        def store(t0, t1, h0, h1):
            nc.sync.dma_start(out=out_view[:, t0:t1, h0:h1], in_=out_sb[:, t0:t1, h0:h1])

        nc.scalar.dma_start(out=bih[:], in_=b_ih0.rearrange("(t p) -> t p", p=P))
        nc.scalar.dma_start(out=bhh[:], in_=b_hh0.rearrange("(t p) -> t p", p=P))
        load_w(0, 0, 1)
        load_w(0, 1, 1)
        load_x(0)
        load_x(1)
        load_w(1, 0, 2)
        load_w(2, 0, 2)
        load_x(2)
        load_x(3)
        for hp in range(1, NH // 2):
            for gi in range(3):
                load_w(gi, 2 * hp, 2)

        make_identity(nc, ident[:])
        nc.vector.memset(warm_in[:], 0.0)
        nc.vector.memset(bsum[:], 0.0)
        nc.scalar.activation(out=warm_out[:], in_=warm_in[:], func=AF.Sigmoid)
        if WARM:
            zeros = keep.tile([P, 512], BF16, name="zeros")
            nc.vector.memset(zeros[:], 0.0)
            ps_warm = bank("m3")

        def dummy(count):
            for k in range(count):
                nc.tensor.matmul(out=ps_warm[:], lhsT=zeros[:, 0:P], rhs=zeros[:], start=True, stop=True)

        dummy(WARM)

        j_w = [("w", gi, 0) for gi in range(3)]
        j_x = [("x", k, 0) for k in range(4)]
        p_wi = prep_transpose(j_w[0], "o1")
        dummy(1)
        p_x0 = prep_transpose(j_x[0], "in0")
        dummy(1)
        p_x1 = prep_transpose(j_x[1], "o0")
        dummy(1)
        nc.vector.tensor_tensor(out=bsum[0:32, :], in0=bih[:], in1=bhh[:], op=ALU.add)
        p_b = bank("c0")
        nc.tensor.transpose(p_b[:, 0:P], bsum[:], ident[:])
        g_wi = prep_copy("v", p_wi)
        g_x0 = prep_copy("s", p_x0)
        prep_quant(j_w[0], g_wi)
        g_x1 = prep_copy("s", p_x1)
        prep_quant(j_x[0], g_x0)
        nc.vector.tensor_copy(out=bias_sb[:], in_=p_b[:, 0:32])
        prep_quant(j_x[1], g_x1)
        p_wg = prep_transpose(j_w[1], "o1")
        g_wg = prep_copy("s", p_wg)
        ia = [mx_pass(0, 0, 0, 256), mx_pass(1, 0, 0, 256)]
        p_wo = prep_transpose(j_w[2], "in0")
        ib = [mx_pass(0, 0, 256, 512), mx_pass(1, 0, 256, 512)]
        act_gate(0, 0, ia[0], 0, 256)
        act_gate(1, 0, ia[1], 0, 256)
        act_gate(0, 0, ib[0], 256, 512)
        act_gate(1, 0, ib[1], 256, 512)
        prep_quant(j_w[1], g_wg)
        g_wo = prep_copy("v", p_wo)
        prep_quant(j_w[2], g_wo)
        gg = [mx_pass(0, 1, 0, 512), mx_pass(1, 1, 0, 512)]
        p_x2 = prep_transpose(j_x[2], "o0")
        act_gate(0, 1, gg[0], 0, 512)
        act_gate(1, 1, gg[1], 0, 512)
        cmult(nc.gpsimd, 0, 0, 512)
        cmult(nc.gpsimd, 1, 0, 512)
        oo = [mx_pass(0, 2, 0, 512), mx_pass(1, 2, 0, 512)]
        p_x3 = prep_transpose(j_x[3], "o1")
        act_gate(0, 2, oo[0], 0, 512)
        act_gate(1, 2, oo[1], 0, 512)
        g_x2 = prep_copy("v", p_x2)
        prep_quant(j_x[2], g_x2)
        g_x3 = prep_copy("v", p_x3)
        prep_quant(j_x[3], g_x3)
        o_ps[0] = back_transpose(acts[(0, 2)], bank("o0"), 0, 4)
        c_ps[0] = back_transpose(c_t[0], bank("c0"), 0, 4)
        j_wi1 = ("w", 0, 1)
        p_wi1 = prep_transpose(j_wi1, "in0")
        act_c(0, c_ps[0], 0, 512)
        nxt = [mx_pass(2, gi, 0, 512) for gi in range(3)]
        pending = [(j_wi1, prep_copy("v", p_wi1))]

        jobs = {2: [(("w", 1, 1), "in0"), (("w", 2, 1), "o0")]}
        for hp in (2, 3):
            for gi in range(3):
                jobs[4 * hp - 4 + gi] = [(("w", gi, hp), "in0")]

        for n in range(2, NU):
            for job, grouped in pending:
                prep_quant(job, grouped)
            pending = []
            final(n - 2, 0, 4)
            ht, grp = units[n - 2]
            if ht % 2 == 1:
                store(4 * grp, 4 * grp + 4, (ht - 1) * P, (ht + 1) * P)
            o_ps[n - 1] = back_transpose(acts[(n - 1, 2)], bank("o%d" % ((n - 1) % 2)), 0, 4)
            banks = [(job, prep_transpose(job, tag)) for job, tag in jobs.get(n, [])]
            c_ps[n - 1] = back_transpose(c_t[n - 1], bank("c0"), 0, 4)
            cur = nxt
            act_gate(n, 0, cur[0], 0, 512)
            act_gate(n, 1, cur[1], 0, 512)
            if n + 1 < NU:
                nxt = [mx_pass(n + 1, gi, 0, 512) for gi in range(3)]
            act_gate(n, 2, cur[2], 0, 512)
            act_c(n - 1, c_ps[n - 1], 0, 512)
            if n < NU - 2:
                cmult(nc.gpsimd, n, 0, 512)
            elif n == NU - 2:
                cmult(nc.vector, n, 0, 512)
            else:
                cmult(nc.vector, n, 0, 256)
                cmult(nc.vector, n, 256, 512)
            for job, ps in banks:
                pending.append((job, prep_copy("v", ps)))

        last = NU - 1
        ht, grp = units[last - 1]
        final(last - 1, 0, 4)
        store(4 * grp, 4 * grp + 4, ht * P, (ht + 1) * P)
        ht, grp = units[last]
        c_a = back_transpose(c_t[last], bank("in0"), 0, 2)
        c_b = back_transpose(c_t[last], mx_bank(), 2, 4)
        o_ps[last] = back_transpose(acts[(last, 2)], bank("o%d" % (last % 2)), 0, 4)
        act_c(last, c_a, 0, 256)
        act_c(last, c_b, 256, 512)
        for t0 in (0, 2):
            final(last, t0, t0 + 2)
            store(4 * grp + t0, 4 * grp + t0 + 2, ht * P, (ht + 1) * P)
